import numpy as np
import ml_dtypes


def mxq(x, axis, fmt="e4m3"):
    dtype, down = {"e4m3": (ml_dtypes.float8_e4m3fn, 7), "e5m2": (ml_dtypes.float8_e5m2, 14)}[fmt]
    v = np.moveaxis(np.asarray(x, np.float32).astype(ml_dtypes.bfloat16).astype(np.float64), axis, -1)
    blocks = v.reshape(v.shape[:-1] + (-1, 32))
    amax = np.abs(blocks).max(-1, keepdims=True)
    byte = np.maximum(np.where(amax > 0, np.frexp(amax)[1] - 1 + 127, 0) - down, 1)
    scale = np.exp2(byte - 127.0)
    codes = (blocks / scale).astype(np.float32).astype(dtype).astype(np.float64)
    return np.moveaxis((codes * scale).reshape(v.shape), -1, axis)


WIDE = False


def mx_kscale(k):
    if not WIDE:
        return np.ones(k)
    levels = np.array([10, -10, 5, -5, 0])
    if k % 512:
        return np.exp2(np.random.permutation(np.resize(levels, k // 32))).repeat(32)
    a = np.empty((k // 512, 16))
    for p in range(k // 512):
        a[p, :8] = np.random.permutation(np.resize(levels, 8))
        for g in range(8):
            far = levels[np.abs(levels - a[p, g]) >= 10]
            a[p, g + 8] = far[np.random.randint(len(far))]
    return np.exp2(a.ravel()).repeat(32)


BF16 = ml_dtypes.bfloat16


def bf(x):
    return np.asarray(x, np.float32).astype(BF16)


def f64(x):
    return np.asarray(x).astype(np.float64)


E2M1 = np.array([0.0, 0.5, 1.0, 1.5, 2.0, 3.0, 4.0, 6.0, -0.0, -0.5, -1.0, -1.5, -2.0, -3.0, -4.0, -6.0])


def pack_weight(w, fmt):
    k, n = w.shape
    w = f64(bf(w)).reshape(k // 32, 32, n)
    amax = np.abs(w).max(1)
    if fmt == "e4m3":
        byte = np.frexp(amax)[1] - 1 + 127 - 7
    else:
        mant, ex = np.frexp(amax / 6.0)
        byte = np.where(mant > 0.5, ex, ex - 1) + 127
    byte = np.clip(np.where(amax > 0, byte, 1), 1, 254)
    scaled = (w * np.exp2(127.0 - byte)[:, None, :]).reshape(k, n).astype(np.float32)
    by_word = np.ascontiguousarray(scaled.reshape(k // 512, 128, 4, n).transpose(0, 1, 3, 2))
    if fmt == "e4m3":
        words = by_word.astype(ml_dtypes.float8_e4m3fn).view(np.uint8)
    else:
        c = by_word.astype(ml_dtypes.float4_e2m1fn).view(np.uint8) & 0xF
        words = c[..., 0::2] | (c[..., 1::2] << 4)
    return np.ascontiguousarray(words), np.ascontiguousarray(byte.astype(np.uint8).reshape(k // 512, 16, n))


def unpack_weight(words, scales, fmt):
    g, p, n, _ = words.shape
    if fmt == "e4m3":
        vals = np.ascontiguousarray(words).view(ml_dtypes.float8_e4m3fn).astype(np.float64)
    else:
        nib = np.empty((g, p, n, 4), np.uint8)
        nib[..., 0::2] = words & 0xF
        nib[..., 1::2] = words >> 4
        vals = E2M1[nib]
    vals = vals * np.repeat(np.exp2(scales.astype(np.float64) - 127.0), 8, axis=1)[..., None]
    return vals.transpose(0, 1, 3, 2).reshape(g * 512, n)


B, C, CI, N = 16, 256, 512, 512
EPS = 1e-5


def setup_inputs():
    s, t = mx_kscale(N), mx_kscale(CI)
    r = np.random.standard_normal
    affinity = bf(r((B, N, N)) * 0.2 * s[None, None, :])
    g_x = bf(r((B, N, CI)) / s[None, :, None] * t[None, None, :])
    w = r((C, CI)) * 1.5 / (0.2 * np.sqrt(N) * np.sqrt(CI)) / t[None, :]
    w_w_words, w_w_scales = pack_weight(np.ascontiguousarray(w.T), "e4m3")
    return {"affinity": affinity,
            "g_x": g_x,
            "w_w_words": w_w_words,
            "w_w_scales": w_w_scales,
            "w_b": bf(r(C) * 0.3),
            "bn_gamma": bf(r(C)),
            "bn_beta": bf(r(C) * 0.5),
            "bn_mean": bf(r(C) * 0.5),
            "bn_var": bf(np.random.uniform(0.5, 1.5, C)),
            "x": bf(r((B, C, N)))}


def reference(affinity, g_x, w_w_words, w_w_scales, w_b, bn_gamma, bn_beta, bn_mean, bn_var, x):
    y = (mxq(f64(affinity), 2, "e4m3") @ mxq(f64(g_x), 1, "e4m3")).transpose(0, 2, 1)
    wy = (unpack_weight(w_w_words, w_w_scales, "e4m3").T @ mxq(y, 1, "e4m3")) + f64(w_b)[None, :, None]
    inv_std = 1.0 / np.sqrt(f64(bn_var) + EPS)
    wy = f64(bn_gamma)[None, :, None] * (wy - f64(bn_mean)[None, :, None]) * inv_std[None, :, None] + f64(bn_beta)[None, :, None]
    return wy + f64(x)

@@ -1,0 +1,227 @@
+from contextlib import ExitStack
+
+import concourse.mybir as mybir
+from concourse.masks import make_identity
+
+F32 = mybir.dt.float32
+BF16 = mybir.dt.bfloat16
+I32 = mybir.dt.int32
+U32 = mybir.dt.uint32
+U8 = mybir.dt.uint8
+FP8X4 = mybir.dt.float8_e4m3fn_x4
+ALU = mybir.AluOpType
+ACT = mybir.ActivationFunctionType
+
+P = 128
+PACK = 4
+B = 16
+N = 512
+CI = 512
+C = 256
+HALVES = C // P
+EPS = 1e-5
+LOOKAHEAD = 5
+
+FLOPS = B * (2 * N * N * CI + 2 * C * CI * N)
+
+
+def tile_sgcam_pb_t_kernel(
+    tc, affinity, g_x, w_w_words, w_w_scales, w_b, bn_gamma, bn_beta, bn_mean, bn_var, x, out
+):
+    nc = tc.nc
+    with ExitStack() as stack:
+        stack.enter_context(tc.manual_schedule())
+        consts = stack.enter_context(tc.tile_pool(name="consts", bufs=1))
+        a_pool = stack.enter_context(tc.tile_pool(name="a_pool", bufs=LOOKAHEAD + 1))
+        g_pool = stack.enter_context(tc.tile_pool(name="g_pool", bufs=LOOKAHEAD + 1))
+        x_pool = stack.enter_context(tc.tile_pool(name="x_pool", bufs=LOOKAHEAD + 2))
+        grouped = stack.enter_context(tc.tile_pool(name="grouped", bufs=3))
+        packed = stack.enter_context(tc.tile_pool(name="packed", bufs=3))
+        res_pool = stack.enter_context(tc.tile_pool(name="res_pool", bufs=4))
+        psum_at = stack.enter_context(tc.psum_pool(name="psum_at", bufs=2))
+        psum_y = stack.enter_context(tc.psum_pool(name="psum_y", bufs=4))
+        psum_wy = stack.enter_context(tc.psum_pool(name="psum_wy", bufs=2))
+
+        live = {}
+
+        ident = consts.tile([P, P], F32)
+        make_identity(nc, ident[:])
+
+        def load_a_g(b):
+            a_sb = a_pool.tile([P, PACK, N], BF16)
+            nc.sync.dma_start(out=a_sb[:], in_=affinity[b].rearrange("(p r) m -> p r m", r=PACK))
+            g_sb = g_pool.tile([P, PACK, CI], BF16)
+            nc.sync.dma_start(out=g_sb[:], in_=g_x[b].rearrange("(p j) c -> p j c", j=PACK))
+            live["a_sb", b] = a_sb
+            live["g_sb", b] = g_sb
+
+        def load_x(b):
+            x_sb = x_pool.tile([P, HALVES, N], BF16)
+            nc.sync.dma_start(out=x_sb[:], in_=x[b].rearrange("(h p) n -> p h n", h=HALVES))
+            live["x_sb", b] = x_sb
+
+        def transpose_affinity(b):
+            a_words = live["a_sb", b][:].bitcast(F32)
+            a_grouped = grouped.tile([P, N, PACK], BF16, align_bytes=64)
+            a_pairs = a_grouped[:].bitcast(F32).rearrange("q (p r) u -> q p r u", r=PACK)
+            for pair in range(2):
+                at = psum_at.tile([P, 2, 2, P], F32, tag="at")
+                for r in range(2):
+                    for u in range(2):
+                        nc.tensor.transpose(
+                            at[:, r, u, :], a_words[:, 2 * pair + r, u : 2 * P : 2], ident[:]
+                        )
+                nc.scalar.copy(
+                    out=a_pairs[:, :, 2 * pair : 2 * pair + 2, :],
+                    in_=at[:].rearrange("q r u p -> q p r u"),
+                )
+            live["a_grouped", b] = a_grouped
+
+        def regroup_values(b):
+            g_grouped = grouped.tile([P, PACK, P, PACK], BF16, align_bytes=64)
+            nc.vector.tensor_copy(
+                out=g_grouped[:].rearrange("q t p j -> q p j t"),
+                in_=live["g_sb", b][:].rearrange("q j (p t) -> q p j t", t=PACK),
+            )
+            live["g_grouped", b] = g_grouped
+
+        def quantise(name, b, flat):
+            codes = packed.tile([P, N], U32, align_bytes=64, tag=name + "_codes", name=name + "_codes")
+            plane = packed.tile([P, N], U8, align_bytes=64, tag=name + "_plane", name=name + "_plane")
+            nc.vector.quantize_mx(out=codes[:].bitcast(FP8X4), scales=plane[:], in_=flat)
+            live[name + "_codes", b] = codes
+            live[name + "_plane", b] = plane
+
+        def aggregate(b):
+            a_codes, a_plane = live["a_codes", b], live["a_plane", b]
+            g_codes, g_plane = live["g_codes", b], live["g_plane", b]
+            y_grouped = grouped.tile([P, N, PACK], BF16, align_bytes=64)
+            for s in range(N // P):
+                n_cols = slice(P * s, P * (s + 1))
+                yt = psum_y.tile([P, PACK, P], F32)
+                for t in range(PACK):
+                    ci_cols = slice(P * t, P * (t + 1))
+                    nc.tensor.matmul_mx(
+                        out=yt[:, t, :],
+                        lhsT=g_codes[:, ci_cols].bitcast(FP8X4),
+                        lhsT_scale=g_plane[:, ci_cols],
+                        rhs=a_codes[:, n_cols].bitcast(FP8X4),
+                        rhs_scale=a_plane[:, n_cols],
+                        start=True,
+                        stop=True,
+                    )
+                nc.scalar.copy(out=y_grouped[:, n_cols, :], in_=yt[:].rearrange("p t n -> p n t"))
+            live["y_grouped", b] = y_grouped
+
+        def project(b):
+            for h in range(HALVES):
+                c_cols = slice(P * h, P * (h + 1))
+                wy = psum_wy.tile([P, N], F32)
+                nc.tensor.matmul_mx(
+                    out=wy[:],
+                    lhsT=w_codes[:, c_cols].bitcast(FP8X4),
+                    lhsT_scale=w_plane[:, c_cols],
+                    rhs=live["y_codes", b][:].bitcast(FP8X4),
+                    rhs_scale=live["y_plane", b][:],
+                    start=True,
+                    stop=True,
+                )
+                live["wy", b, h] = wy
+
+        def shift_residual(b):
+            x_sb = live["x_sb", b]
+            res = res_pool.tile([P, HALVES, N], F32)
+            nc.scalar.activation(
+                out=res[:, 0, :], in_=x_sb[:, 0, :], func=ACT.Identity, bias=shift[:, 0:1], scale=1.0
+            )
+            nc.vector.tensor_scalar_add(out=res[:, 1, :], in0=x_sb[:, 1, :], scalar1=shift[:, 1:2])
+            live["res", b] = res
+
+        def finish(b):
+            res = live["res", b]
+            for h in range(HALVES):
+                nc.vector.scalar_tensor_tensor(
+                    out=res[:, h, :],
+                    in0=live["wy", b, h][:],
+                    scalar=scale[:, h : h + 1],
+                    in1=res[:, h, :],
+                    op0=ALU.mult,
+                    op1=ALU.add,
+                )
+                nc.sync.dma_start(out=out[b, P * h : P * (h + 1), :], in_=res[:, h, :])
+
+        def issue_loads(j):
+            if 0 <= j < B:
+                load_a_g(j)
+            if 0 <= j - 2 < B:
+                load_x(j - 2)
+
+        def step(i):
+            issue_loads(i + 2 + LOOKAHEAD)
+            if 0 <= i - 2 < B:
+                finish(i - 2)
+            if 0 <= i - 1 < B:
+                quantise("y", i - 1, live["y_grouped", i - 1][:].rearrange("p n t -> p (n t)"))
+            if 0 <= i + 2 < B:
+                transpose_affinity(i + 2)
+            if 0 <= i < B:
+                aggregate(i)
+            if 0 <= i - 1 < B:
+                project(i - 1)
+            if 0 <= i + 1 < B:
+                quantise("a", i + 1, live["a_grouped", i + 1][:].rearrange("q n t -> q (n t)"))
+                quantise("g", i + 1, live["g_grouped", i + 1][:].rearrange("q t p j -> q (t p j)"))
+            if 0 <= i + 2 < B:
+                regroup_values(i + 2)
+            if 0 <= i - 1 < B:
+                shift_residual(i - 1)
+
+        vec_rows = consts.tile([P, P], BF16)
+        nc.vector.memset(vec_rows[:], 0.0)
+        for v, vec in enumerate((w_b, bn_gamma, bn_beta, bn_mean, bn_var)):
+            nc.scalar.dma_start(
+                out=vec_rows[HALVES * v : HALVES * (v + 1), :],
+                in_=vec.rearrange("(h p) -> h p", h=HALVES),
+            )
+
+        w_codes = consts.tile([P, C], U32, align_bytes=64)
+        w_plane = consts.tile([P, C], U8, align_bytes=64)
+        nc.vector.memset(w_plane[:].bitcast(I32), 0)
+        issue_loads(0)
+        issue_loads(1)
+        nc.sync.dma_start(
+            out=w_codes[:].bitcast(I32), in_=w_w_words[0].rearrange("p n t -> p (n t)").bitcast(I32)
+        )
+        for quad in range(4):
+            nc.sync.dma_start(
+                out=w_plane[32 * quad : 32 * quad + 4, :].bitcast(I32),
+                in_=w_w_scales[0, 4 * quad : 4 * quad + 4, :].bitcast(I32),
+            )
+        for j in range(2, LOOKAHEAD):
+            issue_loads(j)
+
+        vec_rows_f32 = consts.tile([P, P], F32)
+        nc.vector.tensor_copy(out=vec_rows_f32[:], in_=vec_rows[:])
+        vec_ps = psum_at.tile([P, 2, 2, P], F32, tag="at")
+        nc.tensor.transpose(vec_ps[:, 0, 0, :], vec_rows_f32[:], ident[:])
+        vecs = consts.tile([P, 5, HALVES], F32)
+        nc.vector.tensor_copy(
+            out=vecs[:].rearrange("p v h -> p (v h)"), in_=vec_ps[:, 0, 0, 0 : 5 * HALVES]
+        )
+        bias_c, gamma_c, beta_c, mean_c, var_c = (vecs[:, v, :] for v in range(5))
+        scale = consts.tile([P, HALVES], F32)
+        shift = consts.tile([P, HALVES], F32)
+        nc.vector.tensor_scalar_add(out=scale[:], in0=var_c, scalar1=EPS)
+        nc.scalar.activation(out=scale[:], in_=scale[:], func=ACT.Sqrt)
+
+        step(-2)
+        step(-1)
+
+        nc.vector.reciprocal(out=scale[:], in_=scale[:])
+        nc.vector.tensor_mul(out=scale[:], in0=scale[:], in1=gamma_c)
+        nc.vector.tensor_sub(out=shift[:], in0=bias_c, in1=mean_c)
+        nc.vector.tensor_mul(out=shift[:], in0=shift[:], in1=scale[:])
+        nc.vector.tensor_add(out=shift[:], in0=shift[:], in1=beta_c)
+
+        for i in range(B + 2):
+            step(i)

@@ -131,10 +131,15 @@ def tile_sgcam_pb_t_kernel(
         def shift_residual(b):
             x_sb = live["x_sb", b]
             res = res_pool.tile([P, HALVES, N], F32)
-            nc.scalar.activation(
-                out=res[:, 0, :], in_=x_sb[:, 0, :], func=ACT.Identity, bias=shift[:, 0:1], scale=1.0
-            )
-            nc.vector.tensor_scalar_add(out=res[:, 1, :], in0=x_sb[:, 1, :], scalar1=shift[:, 1:2])
+            for h in range(HALVES):
+                nc.gpsimd.tensor_scalar(
+                    out=res[:, h, :],
+                    in0=x_sb[:, h, :],
+                    scalar1=1.0,
+                    scalar2=shift[:, h : h + 1],
+                    op0=ALU.mult,
+                    op1=ALU.add,
+                )
             live["res", b] = res
 
         def finish(b):

@@ -37,7 +37,7 @@ def tile_sgcam_pb_t_kernel(
         x_pool = stack.enter_context(tc.tile_pool(name="x_pool", bufs=LOOKAHEAD + 2))
         grouped = stack.enter_context(tc.tile_pool(name="grouped", bufs=3))
         packed = stack.enter_context(tc.tile_pool(name="packed", bufs=3))
-        res_pool = stack.enter_context(tc.tile_pool(name="res_pool", bufs=4))
+        res_pool = stack.enter_context(tc.tile_pool(name="res_pool", bufs=12))
         psum_at = stack.enter_context(tc.psum_pool(name="psum_at", bufs=2))
         psum_y = stack.enter_context(tc.psum_pool(name="psum_y", bufs=4))
         psum_wy = stack.enter_context(tc.psum_pool(name="psum_wy", bufs=2))
@@ -57,7 +57,7 @@ def tile_sgcam_pb_t_kernel(
 
         def load_x(b):
             x_sb = x_pool.tile([P, HALVES, N], BF16)
-            nc.sync.dma_start(out=x_sb[:], in_=x[b].rearrange("(h p) n -> p h n", h=HALVES))
+            nc.sync.dma_start(out=x_sb[:], in_=x[b].rearrange("(p h) n -> p h n", h=HALVES))
             live["x_sb", b] = x_sb
 
         def transpose_affinity(b):
@@ -144,6 +144,7 @@ def tile_sgcam_pb_t_kernel(
 
         def finish(b):
             res = live["res", b]
+            out_rows = out[b].rearrange("(p h) n -> p h n", h=HALVES)
             for h in range(HALVES):
                 nc.vector.scalar_tensor_tensor(
                     out=res[:, h, :],
@@ -153,7 +154,10 @@ def tile_sgcam_pb_t_kernel(
                     op0=ALU.mult,
                     op1=ALU.add,
                 )
-                nc.sync.dma_start(out=out[b, P * h : P * (h + 1), :], in_=res[:, h, :])
+                if b == B - 1:
+                    nc.sync.dma_start(out=out_rows[:, h, :], in_=res[:, h, :])
+            if b < B - 1:
+                nc.sync.dma_start(out=out_rows, in_=res[:])
 
         def issue_loads(j):
             if 0 <= j < B:
@@ -181,37 +185,38 @@ def tile_sgcam_pb_t_kernel(
             if 0 <= i - 1 < B:
                 shift_residual(i - 1)
 
-        vec_rows = consts.tile([P, P], BF16)
+        vec_rows = consts.tile([P, C], BF16)
         nc.vector.memset(vec_rows[:], 0.0)
         for v, vec in enumerate((w_b, bn_gamma, bn_beta, bn_mean, bn_var)):
             nc.scalar.dma_start(
-                out=vec_rows[HALVES * v : HALVES * (v + 1), :],
-                in_=vec.rearrange("(h p) -> h p", h=HALVES),
+                out=vec_rows[v : v + 1, :],
+                in_=vec.rearrange("(o c) -> o c", o=1),
             )
 
-        w_codes = consts.tile([P, C], U32, align_bytes=64)
-        w_plane = consts.tile([P, C], U8, align_bytes=64)
-        nc.vector.memset(w_plane[:].bitcast(I32), 0)
+        w_codes_raw = consts.tile([P, C], I32)
+        w_plane_raw = consts.tile([P, C], U8)
+        nc.vector.memset(w_plane_raw[:].bitcast(I32), 0)
         issue_loads(0)
         issue_loads(1)
         nc.sync.dma_start(
-            out=w_codes[:].bitcast(I32), in_=w_w_words[0].rearrange("p n t -> p (n t)").bitcast(I32)
+            out=w_codes_raw[:], in_=w_w_words[0].rearrange("p n t -> p (n t)").bitcast(I32)
         )
         for quad in range(4):
             nc.sync.dma_start(
-                out=w_plane[32 * quad : 32 * quad + 4, :].bitcast(I32),
+                out=w_plane_raw[32 * quad : 32 * quad + 4, :].bitcast(I32),
                 in_=w_w_scales[0, 4 * quad : 4 * quad + 4, :].bitcast(I32),
             )
         for j in range(2, LOOKAHEAD):
             issue_loads(j)
 
-        vec_rows_f32 = consts.tile([P, P], F32)
+        vec_rows_f32 = consts.tile([P, C], F32)
         nc.vector.tensor_copy(out=vec_rows_f32[:], in_=vec_rows[:])
         vec_ps = psum_at.tile([P, 2, 2, P], F32, tag="at")
-        nc.tensor.transpose(vec_ps[:, 0, 0, :], vec_rows_f32[:], ident[:])
+        for h in range(HALVES):
+            nc.tensor.transpose(vec_ps[:, 0, h, :], vec_rows_f32[:, h : C : HALVES], ident[:])
         vecs = consts.tile([P, 5, HALVES], F32)
         nc.vector.tensor_copy(
-            out=vecs[:].rearrange("p v h -> p (v h)"), in_=vec_ps[:, 0, 0, 0 : 5 * HALVES]
+            out=vecs[:], in_=vec_ps[:, 0, :, 0:5].rearrange("p h v -> p v h")
         )
         bias_c, gamma_c, beta_c, mean_c, var_c = (vecs[:, v, :] for v in range(5))
         scale = consts.tile([P, HALVES], F32)
@@ -221,6 +226,17 @@ def tile_sgcam_pb_t_kernel(
 
         step(-2)
         step(-1)
+
+        w_codes = consts.tile([P, C], I32, align_bytes=64)
+        w_plane = consts.tile([P, C], U8, align_bytes=64)
+        nc.vector.tensor_copy(
+            out=w_codes[:].rearrange("p (h q) -> p h q", h=HALVES),
+            in_=w_codes_raw[:].rearrange("p (q h) -> p h q", h=HALVES),
+        )
+        nc.vector.tensor_copy(
+            out=w_plane[:].rearrange("p (h q) -> p h q", h=HALVES),
+            in_=w_plane_raw[:].rearrange("p (q h) -> p h q", h=HALVES),
+        )
 
         nc.vector.reciprocal(out=scale[:], in_=scale[:])
         nc.vector.tensor_mul(out=scale[:], in0=scale[:], in1=gamma_c)

@@ -35,7 +35,7 @@ def tile_sgcam_pb_t_kernel(
         a_pool = stack.enter_context(tc.tile_pool(name="a_pool", bufs=LOOKAHEAD + 1))
         g_pool = stack.enter_context(tc.tile_pool(name="g_pool", bufs=LOOKAHEAD + 1))
         x_pool = stack.enter_context(tc.tile_pool(name="x_pool", bufs=LOOKAHEAD + 2))
-        grouped = stack.enter_context(tc.tile_pool(name="grouped", bufs=3))
+        grouped = stack.enter_context(tc.tile_pool(name="grouped", bufs=4))
         packed = stack.enter_context(tc.tile_pool(name="packed", bufs=3))
         res_pool = stack.enter_context(tc.tile_pool(name="res_pool", bufs=12))
         psum_at = stack.enter_context(tc.psum_pool(name="psum_at", bufs=2))
@@ -60,58 +60,68 @@ def tile_sgcam_pb_t_kernel(
             nc.sync.dma_start(out=x_sb[:], in_=x[b].rearrange("(p h) n -> p h n", h=HALVES))
             live["x_sb", b] = x_sb
 
-        def transpose_affinity(b):
-            a_words = live["a_sb", b][:].bitcast(F32)
-            a_grouped = grouped.tile([P, N, PACK], BF16, align_bytes=64)
-            a_pairs = a_grouped[:].bitcast(F32).rearrange("q (p r) u -> q p r u", r=PACK)
-            for pair in range(2):
-                at = psum_at.tile([P, 2, 2, P], F32, tag="at")
-                for r in range(2):
-                    for u in range(2):
-                        nc.tensor.transpose(
-                            at[:, r, u, :], a_words[:, 2 * pair + r, u : 2 * P : 2], ident[:]
-                        )
-                nc.scalar.copy(
-                    out=a_pairs[:, :, 2 * pair : 2 * pair + 2, :],
-                    in_=at[:].rearrange("q r u p -> q p r u"),
+        def ag_grouped_of(b):
+            if ("ag_grouped", b) not in live:
+                live["ag_grouped", b] = grouped.tile(
+                    [P, 2, PACK * N], BF16, align_bytes=64, name="ag_grouped"
                 )
-            live["a_grouped", b] = a_grouped
+            return live["ag_grouped", b]
+
+        def transpose_affinity(b, pair):
+            a_words = live["a_sb", b][:].bitcast(F32)
+            a_pairs = (
+                ag_grouped_of(b)[:, 0, :].bitcast(F32).rearrange("q (p r u) -> q p r u", r=PACK, u=2)
+            )
+            at = psum_at.tile([P, 2, 2, P], F32, tag="at")
+            for r in range(2):
+                for u in range(2):
+                    nc.tensor.transpose(
+                        at[:, r, u, :], a_words[:, 2 * pair + r, u : 2 * P : 2], ident[:]
+                    )
+            nc.scalar.copy(
+                out=a_pairs[:, :, 2 * pair : 2 * pair + 2, :],
+                in_=at[:].rearrange("q r u p -> q p r u"),
+            )
 
         def regroup_values(b):
-            g_grouped = grouped.tile([P, PACK, P, PACK], BF16, align_bytes=64)
             nc.vector.tensor_copy(
-                out=g_grouped[:].rearrange("q t p j -> q p j t"),
+                out=ag_grouped_of(b)[:, 1, :].rearrange(
+                    "q (t p j) -> q p j t", t=PACK, j=PACK
+                ),
                 in_=live["g_sb", b][:].rearrange("q j (p t) -> q p j t", t=PACK),
             )
-            live["g_grouped", b] = g_grouped
 
         def quantise(name, b, flat):
-            codes = packed.tile([P, N], U32, align_bytes=64, tag=name + "_codes", name=name + "_codes")
-            plane = packed.tile([P, N], U8, align_bytes=64, tag=name + "_plane", name=name + "_plane")
+            width = flat.shape[1] // PACK
+            codes = packed.tile([P, width], U32, align_bytes=64, tag=name + "_codes", name=name + "_codes")
+            plane = packed.tile([P, width], U8, align_bytes=64, tag=name + "_plane", name=name + "_plane")
             nc.vector.quantize_mx(out=codes[:].bitcast(FP8X4), scales=plane[:], in_=flat)
             live[name + "_codes", b] = codes
             live[name + "_plane", b] = plane
 
-        def aggregate(b):
-            a_codes, a_plane = live["a_codes", b], live["a_plane", b]
-            g_codes, g_plane = live["g_codes", b], live["g_plane", b]
-            y_grouped = grouped.tile([P, N, PACK], BF16, align_bytes=64)
-            for s in range(N // P):
-                n_cols = slice(P * s, P * (s + 1))
-                yt = psum_y.tile([P, PACK, P], F32)
-                for t in range(PACK):
-                    ci_cols = slice(P * t, P * (t + 1))
-                    nc.tensor.matmul_mx(
-                        out=yt[:, t, :],
-                        lhsT=g_codes[:, ci_cols].bitcast(FP8X4),
-                        lhsT_scale=g_plane[:, ci_cols],
-                        rhs=a_codes[:, n_cols].bitcast(FP8X4),
-                        rhs_scale=a_plane[:, n_cols],
-                        start=True,
-                        stop=True,
-                    )
-                nc.scalar.copy(out=y_grouped[:, n_cols, :], in_=yt[:].rearrange("p t n -> p n t"))
-            live["y_grouped", b] = y_grouped
+        def open_y(b):
+            live["y_grouped", b] = grouped.tile([P, N, PACK], BF16, align_bytes=64, name="y_grouped")
+
+        def aggregate(b, s):
+            codes, plane = live["ag_codes", b], live["ag_plane", b]
+            n_cols = slice(P * s, P * (s + 1))
+            yt = psum_y.tile([P, PACK, P], F32)
+            for t in range(PACK):
+                ci_cols = slice(N + P * t, N + P * (t + 1))
+                nc.tensor.matmul_mx(
+                    out=yt[:, t, :],
+                    lhsT=codes[:, ci_cols].bitcast(FP8X4),
+                    lhsT_scale=plane[:, ci_cols],
+                    rhs=codes[:, n_cols].bitcast(FP8X4),
+                    rhs_scale=plane[:, n_cols],
+                    start=True,
+                    stop=True,
+                )
+            y_out, y_in = live["y_grouped", b][:, n_cols, :], yt[:].rearrange("p t n -> p n t")
+            if b == B - 1 and s % 2:
+                nc.vector.tensor_copy(out=y_out, in_=y_in)
+            else:
+                nc.scalar.copy(out=y_out, in_=y_in)
 
         def project(b):
             for h in range(HALVES):
@@ -128,19 +138,27 @@ def tile_sgcam_pb_t_kernel(
                 )
                 live["wy", b, h] = wy
 
-        def shift_residual(b):
-            x_sb = live["x_sb", b]
-            res = res_pool.tile([P, HALVES, N], F32)
-            for h in range(HALVES):
-                nc.gpsimd.tensor_scalar(
-                    out=res[:, h, :],
-                    in0=x_sb[:, h, :],
-                    scalar1=1.0,
-                    scalar2=shift[:, h : h + 1],
-                    op0=ALU.mult,
-                    op1=ALU.add,
-                )
+        def shift_residual_scalar(b):
+            res = res_pool.tile([P, HALVES, N], F32, name="res")
+            nc.scalar.activation(
+                out=res[:, 0, :],
+                in_=live["x_sb", b][:, 0, :],
+                func=ACT.Identity,
+                bias=shift[:, 0:1],
+                scale=1.0,
+            )
             live["res", b] = res
+
+        def shift_residual_gpsimd(b, after):
+            nc.gpsimd.tensor_copy(out=marker[:], in_=live["ag_grouped", after][:, 1, 0:1])
+            nc.gpsimd.tensor_scalar(
+                out=live["res", b][:, 1, :],
+                in0=live["x_sb", b][:, 1, :],
+                scalar1=1.0,
+                scalar2=shift[:, 1:2],
+                op0=ALU.mult,
+                op1=ALU.add,
+            )
 
         def finish(b):
             res = live["res", b]
@@ -171,27 +189,29 @@ def tile_sgcam_pb_t_kernel(
                 finish(i - 2)
             if 0 <= i - 1 < B:
                 quantise("y", i - 1, live["y_grouped", i - 1][:].rearrange("p n t -> p (n t)"))
-            if 0 <= i + 2 < B:
-                transpose_affinity(i + 2)
             if 0 <= i < B:
-                aggregate(i)
-            if 0 <= i - 1 < B:
-                project(i - 1)
+                open_y(i)
+            for pair in range(2):
+                if 0 <= i < B:
+                    aggregate(i, 2 * pair)
+                    aggregate(i, 2 * pair + 1)
+                if pair == 1 and 0 <= i - 1 < B:
+                    project(i - 1)
+                if i + 2 < B:
+                    transpose_affinity(i + 2, pair)
+            if 0 <= i < B:
+                shift_residual_scalar(i)
             if 0 <= i + 1 < B:
-                quantise("a", i + 1, live["a_grouped", i + 1][:].rearrange("q n t -> q (n t)"))
-                quantise("g", i + 1, live["g_grouped", i + 1][:].rearrange("q t p j -> q (t p j)"))
-            if 0 <= i + 2 < B:
-                regroup_values(i + 2)
-            if 0 <= i - 1 < B:
-                shift_residual(i - 1)
+                quantise("ag", i + 1, live["ag_grouped", i + 1][:].rearrange("q w k -> q (w k)"))
+            for b in {-2: (0,), -1: (1, 2)}.get(i, (i + 3,)):
+                if b < B:
+                    regroup_values(b)
+            if 0 <= i < B:
+                shift_residual_gpsimd(i, min(i + 3, B - 1))
 
-        vec_rows = consts.tile([P, C], BF16)
-        nc.vector.memset(vec_rows[:], 0.0)
+        vecs = consts.tile([P, 5, 16], BF16)
         for v, vec in enumerate((w_b, bn_gamma, bn_beta, bn_mean, bn_var)):
-            nc.scalar.dma_start(
-                out=vec_rows[v : v + 1, :],
-                in_=vec.rearrange("(o c) -> o c", o=1),
-            )
+            nc.scalar.dma_start(out=vecs[:, v, 0:HALVES], in_=vec.rearrange("(p h) -> p h", h=HALVES))
 
         w_codes_raw = consts.tile([P, C], I32)
         w_plane_raw = consts.tile([P, C], U8)
@@ -209,23 +229,21 @@ def tile_sgcam_pb_t_kernel(
         for j in range(2, LOOKAHEAD):
             issue_loads(j)
 
-        vec_rows_f32 = consts.tile([P, C], F32)
-        nc.vector.tensor_copy(out=vec_rows_f32[:], in_=vec_rows[:])
-        vec_ps = psum_at.tile([P, 2, 2, P], F32, tag="at")
-        for h in range(HALVES):
-            nc.tensor.transpose(vec_ps[:, 0, h, :], vec_rows_f32[:, h : C : HALVES], ident[:])
-        vecs = consts.tile([P, 5, HALVES], F32)
-        nc.vector.tensor_copy(
-            out=vecs[:], in_=vec_ps[:, 0, :, 0:5].rearrange("p h v -> p v h")
-        )
-        bias_c, gamma_c, beta_c, mean_c, var_c = (vecs[:, v, :] for v in range(5))
+        bias_c, gamma_c, beta_c, mean_c, var_c = (vecs[:, v, 0:HALVES] for v in range(5))
         scale = consts.tile([P, HALVES], F32)
         shift = consts.tile([P, HALVES], F32)
-        nc.vector.tensor_scalar_add(out=scale[:], in0=var_c, scalar1=EPS)
-        nc.scalar.activation(out=scale[:], in_=scale[:], func=ACT.Sqrt)
+        minus_half = consts.tile([P, HALVES], F32)
+        marker = consts.tile([P, 1], BF16)
+        nc.gpsimd.memset(minus_half[:], -0.5)
+        nc.gpsimd.tensor_scalar(out=scale[:], in0=var_c, scalar1=EPS, scalar2=None, op0=ALU.add)
+        nc.gpsimd.tensor_tensor(out=scale[:], in0=scale[:], in1=minus_half[:], op=ALU.pow)
+        nc.gpsimd.tensor_tensor(out=scale[:], in0=scale[:], in1=gamma_c, op=ALU.mult)
+        nc.gpsimd.tensor_tensor(out=shift[:], in0=bias_c, in1=mean_c, op=ALU.subtract)
+        nc.gpsimd.tensor_tensor(out=shift[:], in0=shift[:], in1=scale[:], op=ALU.mult)
+        nc.gpsimd.tensor_tensor(out=shift[:], in0=shift[:], in1=beta_c, op=ALU.add)
 
-        step(-2)
-        step(-1)
+        for i in range(-2, 0):
+            step(i)
 
         w_codes = consts.tile([P, C], I32, align_bytes=64)
         w_plane = consts.tile([P, C], U8, align_bytes=64)
@@ -237,12 +255,6 @@ def tile_sgcam_pb_t_kernel(
             out=w_plane[:].rearrange("p (h q) -> p h q", h=HALVES),
             in_=w_plane_raw[:].rearrange("p (q h) -> p h q", h=HALVES),
         )
-
-        nc.vector.reciprocal(out=scale[:], in_=scale[:])
-        nc.vector.tensor_mul(out=scale[:], in0=scale[:], in1=gamma_c)
-        nc.vector.tensor_sub(out=shift[:], in0=bias_c, in1=mean_c)
-        nc.vector.tensor_mul(out=shift[:], in0=shift[:], in1=scale[:])
-        nc.vector.tensor_add(out=shift[:], in0=shift[:], in1=beta_c)
 
         for i in range(B + 2):
             step(i)

@@ -150,7 +150,7 @@ def tile_sgcam_pb_t_kernel(
             live["res", b] = res
 
         def shift_residual_gpsimd(b, after):
-            nc.gpsimd.tensor_copy(out=marker[:], in_=live["ag_grouped", after][:, 1, 0:1])
+            nc.gpsimd.tensor_copy(out=marker[:], in_=live["ag_codes", after][:, 0:1])
             nc.gpsimd.tensor_scalar(
                 out=live["res", b][:, 1, :],
                 in0=live["x_sb", b][:, 1, :],
@@ -207,7 +207,7 @@ def tile_sgcam_pb_t_kernel(
                 if b < B:
                     regroup_values(b)
             if 0 <= i < B:
-                shift_residual_gpsimd(i, min(i + 3, B - 1))
+                shift_residual_gpsimd(i, min(i + 1, B - 1))
 
         vecs = consts.tile([P, 5, 16], BF16)
         for v, vec in enumerate((w_b, bn_gamma, bn_beta, bn_mean, bn_var)):
@@ -233,7 +233,7 @@ def tile_sgcam_pb_t_kernel(
         scale = consts.tile([P, HALVES], F32)
         shift = consts.tile([P, HALVES], F32)
         minus_half = consts.tile([P, HALVES], F32)
-        marker = consts.tile([P, 1], BF16)
+        marker = consts.tile([P, 1], U32)
         nc.gpsimd.memset(minus_half[:], -0.5)
         nc.gpsimd.tensor_scalar(out=scale[:], in0=var_c, scalar1=EPS, scalar2=None, op0=ALU.add)
         nc.gpsimd.tensor_tensor(out=scale[:], in0=scale[:], in1=minus_half[:], op=ALU.pow)

@@ -49,7 +49,11 @@ def tile_sgcam_pb_t_kernel(
 
         def load_a_g(b):
             a_sb = a_pool.tile([P, PACK, N], BF16)
-            nc.sync.dma_start(out=a_sb[:], in_=affinity[b].rearrange("(p r) m -> p r m", r=PACK))
+            a_rows = affinity[b].rearrange("(p r) m -> p r m", r=PACK)
+            pieces = 2 if b == 0 else 1
+            for i in range(pieces):
+                r_part = slice(PACK // pieces * i, PACK // pieces * (i + 1))
+                nc.sync.dma_start(out=a_sb[:, r_part, :], in_=a_rows[:, r_part, :])
             g_sb = g_pool.tile([P, PACK, CI], BF16)
             nc.sync.dma_start(out=g_sb[:], in_=g_x[b].rearrange("(p j) c -> p j c", j=PACK))
             live["a_sb", b] = a_sb
@@ -91,13 +95,30 @@ def tile_sgcam_pb_t_kernel(
                 in_=live["g_sb", b][:].rearrange("q j (p t) -> q p j t", t=PACK),
             )
 
-        def quantise(name, b, flat):
-            width = flat.shape[1] // PACK
-            codes = packed.tile([P, width], U32, align_bytes=64, tag=name + "_codes", name=name + "_codes")
-            plane = packed.tile([P, width], U8, align_bytes=64, tag=name + "_plane", name=name + "_plane")
-            nc.vector.quantize_mx(out=codes[:].bitcast(FP8X4), scales=plane[:], in_=flat)
-            live[name + "_codes", b] = codes
-            live[name + "_plane", b] = plane
+        def quantise_ag(b):
+            codes = packed.tile([P, 2 * N], U32, align_bytes=64, name="ag_codes")
+            plane = packed.tile([P, 2 * N], U8, align_bytes=64, name="ag_plane")
+            nc.vector.quantize_mx(
+                out=codes[:].bitcast(FP8X4),
+                scales=plane[:],
+                in_=live["ag_grouped", b][:].rearrange("q w k -> q (w k)"),
+            )
+            live["ag_codes", b] = codes
+            live["ag_plane", b] = plane
+
+        def parts_of(b):
+            width = N // 2 if b == B - 1 else N
+            return [slice(n, n + width) for n in range(0, N, width)]
+
+        def quantise_y(b, n_cols):
+            if ("y_codes", b) not in live:
+                live["y_codes", b] = packed.tile([P, N], U32, align_bytes=64, name="y_codes")
+                live["y_plane", b] = packed.tile([P, N], U8, align_bytes=64, name="y_plane")
+            nc.vector.quantize_mx(
+                out=live["y_codes", b][:, n_cols].bitcast(FP8X4),
+                scales=live["y_plane", b][:, n_cols],
+                in_=live["y_grouped", b][:, n_cols, :].rearrange("p n t -> p (n t)"),
+            )
 
         def open_y(b):
             live["y_grouped", b] = grouped.tile([P, N, PACK], BF16, align_bytes=64, name="y_grouped")
@@ -118,25 +139,25 @@ def tile_sgcam_pb_t_kernel(
                     stop=True,
                 )
             y_out, y_in = live["y_grouped", b][:, n_cols, :], yt[:].rearrange("p t n -> p n t")
-            if b == B - 1 and s % 2:
+            if b == B - 1 and s == 1:
                 nc.vector.tensor_copy(out=y_out, in_=y_in)
             else:
                 nc.scalar.copy(out=y_out, in_=y_in)
 
-        def project(b):
+        def project(b, n_cols):
             for h in range(HALVES):
                 c_cols = slice(P * h, P * (h + 1))
-                wy = psum_wy.tile([P, N], F32)
+                if ("wy", b, h) not in live:
+                    live["wy", b, h] = psum_wy.tile([P, N], F32, name="wy")
                 nc.tensor.matmul_mx(
-                    out=wy[:],
+                    out=live["wy", b, h][:, n_cols],
                     lhsT=w_codes[:, c_cols].bitcast(FP8X4),
                     lhsT_scale=w_plane[:, c_cols],
-                    rhs=live["y_codes", b][:].bitcast(FP8X4),
-                    rhs_scale=live["y_plane", b][:],
+                    rhs=live["y_codes", b][:, n_cols].bitcast(FP8X4),
+                    rhs_scale=live["y_plane", b][:, n_cols],
                     start=True,
                     stop=True,
                 )
-                live["wy", b, h] = wy
 
         def shift_residual_scalar(b):
             res = res_pool.tile([P, HALVES, N], F32, name="res")
@@ -160,22 +181,20 @@ def tile_sgcam_pb_t_kernel(
                 op1=ALU.add,
             )
 
-        def finish(b):
+        def finish(b, n_cols):
             res = live["res", b]
-            out_rows = out[b].rearrange("(p h) n -> p h n", h=HALVES)
             for h in range(HALVES):
                 nc.vector.scalar_tensor_tensor(
-                    out=res[:, h, :],
-                    in0=live["wy", b, h][:],
+                    out=res[:, h, n_cols],
+                    in0=live["wy", b, h][:, n_cols],
                     scalar=scale[:, h : h + 1],
-                    in1=res[:, h, :],
+                    in1=res[:, h, n_cols],
                     op0=ALU.mult,
                     op1=ALU.add,
                 )
-                if b == B - 1:
-                    nc.sync.dma_start(out=out_rows[:, h, :], in_=res[:, h, :])
-            if b < B - 1:
-                nc.sync.dma_start(out=out_rows, in_=res[:])
+            nc.sync.dma_start(
+                out=out[b].rearrange("(p h) n -> p h n", h=HALVES)[:, :, n_cols], in_=res[:, :, n_cols]
+            )
 
         def issue_loads(j):
             if 0 <= j < B:
@@ -185,10 +204,15 @@ def tile_sgcam_pb_t_kernel(
 
         def step(i):
             issue_loads(i + 2 + LOOKAHEAD)
-            if 0 <= i - 2 < B:
-                finish(i - 2)
+            if i == B:
+                quantise_y(B - 1, parts_of(B - 1)[0])
+            if 0 <= i - 2 < B - 1:
+                finish(i - 2, parts_of(i - 2)[0])
             if 0 <= i - 1 < B:
-                quantise("y", i - 1, live["y_grouped", i - 1][:].rearrange("p n t -> p (n t)"))
+                quantise_y(i - 1, parts_of(i - 1)[-1])
+            if i == B + 1:
+                for n_cols in parts_of(B - 1):
+                    finish(B - 1, n_cols)
             if 0 <= i < B:
                 open_y(i)
             for pair in range(2):
@@ -196,14 +220,15 @@ def tile_sgcam_pb_t_kernel(
                     aggregate(i, 2 * pair)
                     aggregate(i, 2 * pair + 1)
                 if pair == 1 and 0 <= i - 1 < B:
-                    project(i - 1)
+                    for n_cols in parts_of(i - 1):
+                        project(i - 1, n_cols)
                 if i + 2 < B:
                     transpose_affinity(i + 2, pair)
             if 0 <= i < B:
                 shift_residual_scalar(i)
             if 0 <= i + 1 < B:
-                quantise("ag", i + 1, live["ag_grouped", i + 1][:].rearrange("q w k -> q (w k)"))
-            for b in {-2: (0,), -1: (1, 2)}.get(i, (i + 3,)):
+                quantise_ag(i + 1)
+            for b in {-2: (0,), -1: (1,), 0: (2, 3)}.get(i, (i + 3,)):
                 if b < B:
                     regroup_values(b)
             if 0 <= i < B:
@@ -216,8 +241,8 @@ def tile_sgcam_pb_t_kernel(
         w_codes_raw = consts.tile([P, C], I32)
         w_plane_raw = consts.tile([P, C], U8)
         nc.vector.memset(w_plane_raw[:].bitcast(I32), 0)
-        issue_loads(0)
-        issue_loads(1)
+        for j in range(3):
+            issue_loads(j)
         nc.sync.dma_start(
             out=w_codes_raw[:], in_=w_w_words[0].rearrange("p n t -> p (n t)").bitcast(I32)
         )
@@ -226,7 +251,7 @@ def tile_sgcam_pb_t_kernel(
                 out=w_plane_raw[32 * quad : 32 * quad + 4, :].bitcast(I32),
                 in_=w_w_scales[0, 4 * quad : 4 * quad + 4, :].bitcast(I32),
             )
-        for j in range(2, LOOKAHEAD):
+        for j in range(3, LOOKAHEAD):
             issue_loads(j)
 
         bias_c, gamma_c, beta_c, mean_c, var_c = (vecs[:, v, 0:HALVES] for v in range(5))
@@ -242,19 +267,17 @@ def tile_sgcam_pb_t_kernel(
         nc.gpsimd.tensor_tensor(out=shift[:], in0=shift[:], in1=scale[:], op=ALU.mult)
         nc.gpsimd.tensor_tensor(out=shift[:], in0=shift[:], in1=beta_c, op=ALU.add)
 
-        for i in range(-2, 0):
-            step(i)
-
         w_codes = consts.tile([P, C], I32, align_bytes=64)
         w_plane = consts.tile([P, C], U8, align_bytes=64)
-        nc.vector.tensor_copy(
+        nc.gpsimd.tensor_copy(
             out=w_codes[:].rearrange("p (h q) -> p h q", h=HALVES),
             in_=w_codes_raw[:].rearrange("p (q h) -> p h q", h=HALVES),
         )
-        nc.vector.tensor_copy(
+        nc.gpsimd.tensor_copy(
             out=w_plane[:].rearrange("p (h q) -> p h q", h=HALVES),
             in_=w_plane_raw[:].rearrange("p (q h) -> p h q", h=HALVES),
         )
 
-        for i in range(B + 2):
+
+        for i in range(-2, B + 2):
             step(i)

@@ -20,6 +20,8 @@ CI = 512
 C = 256
 HALVES = C // P
 EPS = 1e-5
+G_TENSOR = 24
+X_GPSIMD = 192
 LOOKAHEAD = 5
 
 FLOPS = B * (2 * N * N * CI + 2 * C * CI * N)
@@ -39,23 +41,28 @@ def tile_sgcam_pb_t_kernel(
         packed = stack.enter_context(tc.tile_pool(name="packed", bufs=3))
         res_pool = stack.enter_context(tc.tile_pool(name="res_pool", bufs=12))
         psum_at = stack.enter_context(tc.psum_pool(name="psum_at", bufs=2))
-        psum_y = stack.enter_context(tc.psum_pool(name="psum_y", bufs=4))
+        psum_y = stack.enter_context(tc.psum_pool(name="psum_y", bufs=3))
+        psum_g = stack.enter_context(tc.psum_pool(name="psum_g", bufs=1))
         psum_wy = stack.enter_context(tc.psum_pool(name="psum_wy", bufs=2))
 
         live = {}
 
         ident = consts.tile([P, P], F32)
         make_identity(nc, ident[:])
+        ident_bf16 = consts.tile([P, P], BF16)
+        make_identity(nc, ident_bf16[:])
 
         def load_a_g(b):
             a_sb = a_pool.tile([P, PACK, N], BF16)
             a_rows = affinity[b].rearrange("(p r) m -> p r m", r=PACK)
+            g_sb = g_pool.tile([P, PACK, CI], BF16)
+            g_rows = g_x[b].rearrange("(p j) c -> p j c", j=PACK)
             pieces = 2 if b == 0 else 1
             for i in range(pieces):
                 r_part = slice(PACK // pieces * i, PACK // pieces * (i + 1))
+                c_part = slice(CI // pieces * i, CI // pieces * (i + 1))
                 nc.sync.dma_start(out=a_sb[:, r_part, :], in_=a_rows[:, r_part, :])
-            g_sb = g_pool.tile([P, PACK, CI], BF16)
-            nc.sync.dma_start(out=g_sb[:], in_=g_x[b].rearrange("(p j) c -> p j c", j=PACK))
+                nc.sync.dma_start(out=g_sb[:, :, c_part], in_=g_rows[:, :, c_part])
             live["a_sb", b] = a_sb
             live["g_sb", b] = g_sb
 
@@ -87,13 +94,26 @@ def tile_sgcam_pb_t_kernel(
                 in_=at[:].rearrange("q r u p -> q p r u"),
             )
 
-        def regroup_values(b):
-            nc.vector.tensor_copy(
-                out=ag_grouped_of(b)[:, 1, :].rearrange(
-                    "q (t p j) -> q p j t", t=PACK, j=PACK
-                ),
-                in_=live["g_sb", b][:].rearrange("q j (p t) -> q p j t", t=PACK),
+        v_cols = P - G_TENSOR
+
+        def regroup_vector(b):
+            g_out = ag_grouped_of(b)[:, 1, :].rearrange("q (t p j) -> q p j t", t=PACK, j=PACK)
+            g_in = live["g_sb", b][:].rearrange("q j (p t) -> q p j t", t=PACK)
+            edges = (0, P // 2, v_cols) if b == 0 else (0, v_cols)
+            for lo, hi in zip(edges, edges[1:]):
+                nc.vector.tensor_copy(out=g_out[:, lo:hi], in_=g_in[:, lo:hi])
+
+        def regroup_tensor(b):
+            gm = psum_g.tile([P, PACK, G_TENSOR, PACK], BF16)
+            nc.tensor.matmul(
+                out=gm[:],
+                lhsT=ident_bf16[:],
+                rhs=live["g_sb", b][:].rearrange("q j (p t) -> q t p j", t=PACK)[:, :, v_cols:P, :],
+                start=True,
+                stop=True,
             )
+            g_out = ag_grouped_of(b)[:, 1, :].rearrange("q (t p j) -> q t p j", t=PACK, j=PACK)
+            nc.scalar.copy(out=g_out[:, :, v_cols:P, :], in_=gm[:])
 
         def quantise_ag(b):
             codes = packed.tile([P, 2 * N], U32, align_bytes=64, name="ag_codes")
@@ -105,6 +125,16 @@ def tile_sgcam_pb_t_kernel(
             )
             live["ag_codes", b] = codes
             live["ag_plane", b] = plane
+
+        def permute_weight():
+            nc.vector.tensor_copy(
+                out=w_codes[:].rearrange("p (h q) -> p h q", h=HALVES),
+                in_=w_codes_raw[:].rearrange("p (q h) -> p h q", h=HALVES),
+            )
+            nc.vector.tensor_copy(
+                out=w_plane[:].rearrange("p (h q) -> p h q", h=HALVES),
+                in_=w_plane_raw[:].rearrange("p (q h) -> p h q", h=HALVES),
+            )
 
         def parts_of(b):
             width = N // 2 if b == B - 1 else N
@@ -139,10 +169,7 @@ def tile_sgcam_pb_t_kernel(
                     stop=True,
                 )
             y_out, y_in = live["y_grouped", b][:, n_cols, :], yt[:].rearrange("p t n -> p n t")
-            if b == B - 1 and s == 1:
-                nc.vector.tensor_copy(out=y_out, in_=y_in)
-            else:
-                nc.scalar.copy(out=y_out, in_=y_in)
+            nc.scalar.copy(out=y_out, in_=y_in)
 
         def project(b, n_cols):
             for h in range(HALVES):
@@ -159,26 +186,27 @@ def tile_sgcam_pb_t_kernel(
                     stop=True,
                 )
 
+        def shift_residual_gpsimd(b, after):
+            nc.gpsimd.tensor_copy(out=marker[:], in_=live["ag_codes", after][:, 0:1])
+            live["res", b] = res_pool.tile([P, HALVES, N], F32, name="res")
+            for h, n_cols in ((0, slice(N - X_GPSIMD, N)), (1, slice(0, N))):
+                nc.gpsimd.tensor_scalar(
+                    out=live["res", b][:, h, n_cols],
+                    in0=live["x_sb", b][:, h, n_cols],
+                    scalar1=1.0,
+                    scalar2=shift[:, h : h + 1],
+                    op0=ALU.mult,
+                    op1=ALU.add,
+                )
+
         def shift_residual_scalar(b):
-            res = res_pool.tile([P, HALVES, N], F32, name="res")
+            n_cols = slice(0, N - X_GPSIMD)
             nc.scalar.activation(
-                out=res[:, 0, :],
-                in_=live["x_sb", b][:, 0, :],
+                out=live["res", b][:, 0, n_cols],
+                in_=live["x_sb", b][:, 0, n_cols],
                 func=ACT.Identity,
                 bias=shift[:, 0:1],
                 scale=1.0,
-            )
-            live["res", b] = res
-
-        def shift_residual_gpsimd(b, after):
-            nc.gpsimd.tensor_copy(out=marker[:], in_=live["ag_codes", after][:, 0:1])
-            nc.gpsimd.tensor_scalar(
-                out=live["res", b][:, 1, :],
-                in0=live["x_sb", b][:, 1, :],
-                scalar1=1.0,
-                scalar2=shift[:, 1:2],
-                op0=ALU.mult,
-                op1=ALU.add,
             )
 
         def finish(b, n_cols):
@@ -199,11 +227,12 @@ def tile_sgcam_pb_t_kernel(
         def issue_loads(j):
             if 0 <= j < B:
                 load_a_g(j)
-            if 0 <= j - 2 < B:
-                load_x(j - 2)
+            if 0 <= j - 3 < B:
+                load_x(j - 3)
 
         def step(i):
             issue_loads(i + 2 + LOOKAHEAD)
+            regrouped = {-2: (0,), -1: (1,), 0: (2, 3)}.get(i, (i + 3,) if i + 3 < B else ())
             if i == B:
                 quantise_y(B - 1, parts_of(B - 1)[0])
             if 0 <= i - 2 < B - 1:
@@ -213,33 +242,42 @@ def tile_sgcam_pb_t_kernel(
             if i == B + 1:
                 for n_cols in parts_of(B - 1):
                     finish(B - 1, n_cols)
+            if 0 <= i - 1 < B:
+                shift_residual_scalar(i - 1)
             if 0 <= i < B:
                 open_y(i)
             for pair in range(2):
                 if 0 <= i < B:
                     aggregate(i, 2 * pair)
                     aggregate(i, 2 * pair + 1)
+                if pair == 1 and i > 0:
+                    for b in regrouped:
+                        regroup_tensor(b)
                 if pair == 1 and 0 <= i - 1 < B:
                     for n_cols in parts_of(i - 1):
                         project(i - 1, n_cols)
                 if i + 2 < B:
                     transpose_affinity(i + 2, pair)
-            if 0 <= i < B:
-                shift_residual_scalar(i)
             if 0 <= i + 1 < B:
                 quantise_ag(i + 1)
-            for b in {-2: (0,), -1: (1,), 0: (2, 3)}.get(i, (i + 3,)):
-                if b < B:
-                    regroup_values(b)
+            for b in regrouped:
+                if i <= 0:
+                    regroup_tensor(b)
+                regroup_vector(b)
+                if b == 2:
+                    permute_weight()
             if 0 <= i < B:
                 shift_residual_gpsimd(i, min(i + 1, B - 1))
 
         vecs = consts.tile([P, 5, 16], BF16)
         for v, vec in enumerate((w_b, bn_gamma, bn_beta, bn_mean, bn_var)):
-            nc.scalar.dma_start(out=vecs[:, v, 0:HALVES], in_=vec.rearrange("(p h) -> p h", h=HALVES))
+            queue = nc.gpsimd if v % 2 == 0 and v < 4 else nc.scalar
+            queue.dma_start(out=vecs[:, v, 0:HALVES], in_=vec.rearrange("(p h) -> p h", h=HALVES))
 
         w_codes_raw = consts.tile([P, C], I32)
         w_plane_raw = consts.tile([P, C], U8)
+        w_codes = consts.tile([P, C], I32, align_bytes=64)
+        w_plane = consts.tile([P, C], U8, align_bytes=64)
         nc.vector.memset(w_plane_raw[:].bitcast(I32), 0)
         for j in range(3):
             issue_loads(j)
@@ -266,17 +304,6 @@ def tile_sgcam_pb_t_kernel(
         nc.gpsimd.tensor_tensor(out=shift[:], in0=bias_c, in1=mean_c, op=ALU.subtract)
         nc.gpsimd.tensor_tensor(out=shift[:], in0=shift[:], in1=scale[:], op=ALU.mult)
         nc.gpsimd.tensor_tensor(out=shift[:], in0=shift[:], in1=beta_c, op=ALU.add)
-
-        w_codes = consts.tile([P, C], I32, align_bytes=64)
-        w_plane = consts.tile([P, C], U8, align_bytes=64)
-        nc.gpsimd.tensor_copy(
-            out=w_codes[:].rearrange("p (h q) -> p h q", h=HALVES),
-            in_=w_codes_raw[:].rearrange("p (q h) -> p h q", h=HALVES),
-        )
-        nc.gpsimd.tensor_copy(
-            out=w_plane[:].rearrange("p (h q) -> p h q", h=HALVES),
-            in_=w_plane_raw[:].rearrange("p (q h) -> p h q", h=HALVES),
-        )
 
 
         for i in range(-2, B + 2):

@@ -20,8 +20,7 @@ CI = 512
 C = 256
 HALVES = C // P
 EPS = 1e-5
-G_TENSOR = 24
-X_GPSIMD = 192
+G_TENSOR = 12
 LOOKAHEAD = 5
 
 FLOPS = B * (2 * N * N * CI + 2 * C * CI * N)
@@ -41,8 +40,7 @@ def tile_sgcam_pb_t_kernel(
         packed = stack.enter_context(tc.tile_pool(name="packed", bufs=3))
         res_pool = stack.enter_context(tc.tile_pool(name="res_pool", bufs=12))
         psum_at = stack.enter_context(tc.psum_pool(name="psum_at", bufs=2))
-        psum_y = stack.enter_context(tc.psum_pool(name="psum_y", bufs=3))
-        psum_g = stack.enter_context(tc.psum_pool(name="psum_g", bufs=1))
+        psum_y = stack.enter_context(tc.psum_pool(name="psum_y", bufs=4))
         psum_wy = stack.enter_context(tc.psum_pool(name="psum_wy", bufs=2))
 
         live = {}
@@ -104,7 +102,7 @@ def tile_sgcam_pb_t_kernel(
                 nc.vector.tensor_copy(out=g_out[:, lo:hi], in_=g_in[:, lo:hi])
 
         def regroup_tensor(b):
-            gm = psum_g.tile([P, PACK, G_TENSOR, PACK], BF16)
+            gm = psum_at.tile([P, PACK, G_TENSOR, PACK], BF16, tag="at")
             nc.tensor.matmul(
                 out=gm[:],
                 lhsT=ident_bf16[:],
@@ -189,21 +187,19 @@ def tile_sgcam_pb_t_kernel(
         def shift_residual_gpsimd(b, after):
             nc.gpsimd.tensor_copy(out=marker[:], in_=live["ag_codes", after][:, 0:1])
             live["res", b] = res_pool.tile([P, HALVES, N], F32, name="res")
-            for h, n_cols in ((0, slice(N - X_GPSIMD, N)), (1, slice(0, N))):
-                nc.gpsimd.tensor_scalar(
-                    out=live["res", b][:, h, n_cols],
-                    in0=live["x_sb", b][:, h, n_cols],
-                    scalar1=1.0,
-                    scalar2=shift[:, h : h + 1],
-                    op0=ALU.mult,
-                    op1=ALU.add,
-                )
+            nc.gpsimd.tensor_scalar(
+                out=live["res", b][:, 1, :],
+                in0=live["x_sb", b][:, 1, :],
+                scalar1=1.0,
+                scalar2=shift[:, 1:2],
+                op0=ALU.mult,
+                op1=ALU.add,
+            )
 
         def shift_residual_scalar(b):
-            n_cols = slice(0, N - X_GPSIMD)
             nc.scalar.activation(
-                out=live["res", b][:, 0, n_cols],
-                in_=live["x_sb", b][:, 0, n_cols],
+                out=live["res", b][:, 0, :],
+                in_=live["x_sb", b][:, 0, :],
                 func=ACT.Identity,
                 bias=shift[:, 0:1],
                 scale=1.0,

from contextlib import ExitStack

import concourse.mybir as mybir
from concourse.masks import make_identity

F32 = mybir.dt.float32
BF16 = mybir.dt.bfloat16
I32 = mybir.dt.int32
U32 = mybir.dt.uint32
U8 = mybir.dt.uint8
FP8X4 = mybir.dt.float8_e4m3fn_x4
ALU = mybir.AluOpType
ACT = mybir.ActivationFunctionType

P = 128
PACK = 4
B = 16
N = 512
CI = 512
C = 256
HALVES = C // P
EPS = 1e-5
G_TENSOR = 12
LOOKAHEAD = 5

FLOPS = B * (2 * N * N * CI + 2 * C * CI * N)


def tile_sgcam_pb_t_kernel(
    tc, affinity, g_x, w_w_words, w_w_scales, w_b, bn_gamma, bn_beta, bn_mean, bn_var, x, out
):
    nc = tc.nc
    with ExitStack() as stack:
        stack.enter_context(tc.manual_schedule())
        consts = stack.enter_context(tc.tile_pool(name="consts", bufs=1))
        a_pool = stack.enter_context(tc.tile_pool(name="a_pool", bufs=LOOKAHEAD + 1))
        g_pool = stack.enter_context(tc.tile_pool(name="g_pool", bufs=LOOKAHEAD + 1))
        x_pool = stack.enter_context(tc.tile_pool(name="x_pool", bufs=LOOKAHEAD + 2))
        grouped = stack.enter_context(tc.tile_pool(name="grouped", bufs=4))
        packed = stack.enter_context(tc.tile_pool(name="packed", bufs=3))
        res_pool = stack.enter_context(tc.tile_pool(name="res_pool", bufs=12))
        psum_at = stack.enter_context(tc.psum_pool(name="psum_at", bufs=2))
        psum_y = stack.enter_context(tc.psum_pool(name="psum_y", bufs=4))
        psum_wy = stack.enter_context(tc.psum_pool(name="psum_wy", bufs=2))

        live = {}

        ident = consts.tile([P, P], F32)
        make_identity(nc, ident[:])
        ident_bf16 = consts.tile([P, P], BF16)
        make_identity(nc, ident_bf16[:])

        def load_a_g(b):
            a_sb = a_pool.tile([P, PACK, N], BF16)
            a_rows = affinity[b].rearrange("(p r) m -> p r m", r=PACK)
            g_sb = g_pool.tile([P, PACK, CI], BF16)
            g_rows = g_x[b].rearrange("(p j) c -> p j c", j=PACK)
            pieces = 2 if b == 0 else 1
            for i in range(pieces):
                r_part = slice(PACK // pieces * i, PACK // pieces * (i + 1))
                c_part = slice(CI // pieces * i, CI // pieces * (i + 1))
                nc.sync.dma_start(out=a_sb[:, r_part, :], in_=a_rows[:, r_part, :])
                nc.sync.dma_start(out=g_sb[:, :, c_part], in_=g_rows[:, :, c_part])
            live["a_sb", b] = a_sb
            live["g_sb", b] = g_sb

        def load_x(b):
            x_sb = x_pool.tile([P, HALVES, N], BF16)
            nc.sync.dma_start(out=x_sb[:], in_=x[b].rearrange("(p h) n -> p h n", h=HALVES))
            live["x_sb", b] = x_sb

        def ag_grouped_of(b):
            if ("ag_grouped", b) not in live:
                live["ag_grouped", b] = grouped.tile(
                    [P, 2, PACK * N], BF16, align_bytes=64, name="ag_grouped"
                )
            return live["ag_grouped", b]

        def transpose_affinity(b, pair):
            a_words = live["a_sb", b][:].bitcast(F32)
            a_pairs = (
                ag_grouped_of(b)[:, 0, :].bitcast(F32).rearrange("q (p r u) -> q p r u", r=PACK, u=2)
            )
            at = psum_at.tile([P, 2, 2, P], F32, tag="at")
            for r in range(2):
                for u in range(2):
                    nc.tensor.transpose(
                        at[:, r, u, :], a_words[:, 2 * pair + r, u : 2 * P : 2], ident[:]
                    )
            nc.scalar.copy(
                out=a_pairs[:, :, 2 * pair : 2 * pair + 2, :],
                in_=at[:].rearrange("q r u p -> q p r u"),
            )

        v_cols = P - G_TENSOR

        def regroup_vector(b):
            g_out = ag_grouped_of(b)[:, 1, :].rearrange("q (t p j) -> q p j t", t=PACK, j=PACK)
            g_in = live["g_sb", b][:].rearrange("q j (p t) -> q p j t", t=PACK)
            edges = (0, P // 2, v_cols) if b == 0 else (0, v_cols)
            for lo, hi in zip(edges, edges[1:]):
                nc.vector.tensor_copy(out=g_out[:, lo:hi], in_=g_in[:, lo:hi])

        def regroup_tensor(b):
            gm = psum_at.tile([P, PACK, G_TENSOR, PACK], BF16, tag="at")
            nc.tensor.matmul(
                out=gm[:],
                lhsT=ident_bf16[:],
                rhs=live["g_sb", b][:].rearrange("q j (p t) -> q t p j", t=PACK)[:, :, v_cols:P, :],
                start=True,
                stop=True,
            )
            g_out = ag_grouped_of(b)[:, 1, :].rearrange("q (t p j) -> q t p j", t=PACK, j=PACK)
            nc.scalar.copy(out=g_out[:, :, v_cols:P, :], in_=gm[:])

        def quantise_ag(b):
            codes = packed.tile([P, 2 * N], U32, align_bytes=64, name="ag_codes")
            plane = packed.tile([P, 2 * N], U8, align_bytes=64, name="ag_plane")
            nc.vector.quantize_mx(
                out=codes[:].bitcast(FP8X4),
                scales=plane[:],
                in_=live["ag_grouped", b][:].rearrange("q w k -> q (w k)"),
            )
            live["ag_codes", b] = codes
            live["ag_plane", b] = plane

        def permute_weight():
            nc.vector.tensor_copy(
                out=w_codes[:].rearrange("p (h q) -> p h q", h=HALVES),
                in_=w_codes_raw[:].rearrange("p (q h) -> p h q", h=HALVES),
            )
            nc.vector.tensor_copy(
                out=w_plane[:].rearrange("p (h q) -> p h q", h=HALVES),
                in_=w_plane_raw[:].rearrange("p (q h) -> p h q", h=HALVES),
            )

        def parts_of(b):
            width = N // 2 if b == B - 1 else N
            return [slice(n, n + width) for n in range(0, N, width)]

        def quantise_y(b, n_cols):
            if ("y_codes", b) not in live:
                live["y_codes", b] = packed.tile([P, N], U32, align_bytes=64, name="y_codes")
                live["y_plane", b] = packed.tile([P, N], U8, align_bytes=64, name="y_plane")
            nc.vector.quantize_mx(
                out=live["y_codes", b][:, n_cols].bitcast(FP8X4),
                scales=live["y_plane", b][:, n_cols],
                in_=live["y_grouped", b][:, n_cols, :].rearrange("p n t -> p (n t)"),
            )

        def open_y(b):
            live["y_grouped", b] = grouped.tile([P, N, PACK], BF16, align_bytes=64, name="y_grouped")

        def aggregate(b, s):
            codes, plane = live["ag_codes", b], live["ag_plane", b]
            n_cols = slice(P * s, P * (s + 1))
            yt = psum_y.tile([P, PACK, P], F32)
            for t in range(PACK):
                ci_cols = slice(N + P * t, N + P * (t + 1))
                nc.tensor.matmul_mx(
                    out=yt[:, t, :],
                    lhsT=codes[:, ci_cols].bitcast(FP8X4),
                    lhsT_scale=plane[:, ci_cols],
                    rhs=codes[:, n_cols].bitcast(FP8X4),
                    rhs_scale=plane[:, n_cols],
                    start=True,
                    stop=True,
                )
            y_out, y_in = live["y_grouped", b][:, n_cols, :], yt[:].rearrange("p t n -> p n t")
            nc.scalar.copy(out=y_out, in_=y_in)

        def project(b, n_cols):
            for h in range(HALVES):
                c_cols = slice(P * h, P * (h + 1))
                if ("wy", b, h) not in live:
                    live["wy", b, h] = psum_wy.tile([P, N], F32, name="wy")
                nc.tensor.matmul_mx(
                    out=live["wy", b, h][:, n_cols],
                    lhsT=w_codes[:, c_cols].bitcast(FP8X4),
                    lhsT_scale=w_plane[:, c_cols],
                    rhs=live["y_codes", b][:, n_cols].bitcast(FP8X4),
                    rhs_scale=live["y_plane", b][:, n_cols],
                    start=True,
                    stop=True,
                )

        def shift_residual_gpsimd(b, after):
            nc.gpsimd.tensor_copy(out=marker[:], in_=live["ag_codes", after][:, 0:1])
            live["res", b] = res_pool.tile([P, HALVES, N], F32, name="res")
            nc.gpsimd.tensor_scalar(
                out=live["res", b][:, 1, :],
                in0=live["x_sb", b][:, 1, :],
                scalar1=1.0,
                scalar2=shift[:, 1:2],
                op0=ALU.mult,
                op1=ALU.add,
            )

        def shift_residual_scalar(b):
            nc.scalar.activation(
                out=live["res", b][:, 0, :],
                in_=live["x_sb", b][:, 0, :],
                func=ACT.Identity,
                bias=shift[:, 0:1],
                scale=1.0,
            )

        def finish(b, n_cols):
            res = live["res", b]
            for h in range(HALVES):
                nc.vector.scalar_tensor_tensor(
                    out=res[:, h, n_cols],
                    in0=live["wy", b, h][:, n_cols],
                    scalar=scale[:, h : h + 1],
                    in1=res[:, h, n_cols],
                    op0=ALU.mult,
                    op1=ALU.add,
                )
            nc.sync.dma_start(
                out=out[b].rearrange("(p h) n -> p h n", h=HALVES)[:, :, n_cols], in_=res[:, :, n_cols]
            )

        def issue_loads(j):
            if 0 <= j < B:
                load_a_g(j)
            if 0 <= j - 3 < B:
                load_x(j - 3)

        def step(i):
            issue_loads(i + 2 + LOOKAHEAD)
            regrouped = {-2: (0,), -1: (1,), 0: (2, 3)}.get(i, (i + 3,) if i + 3 < B else ())
            if i == B:
                quantise_y(B - 1, parts_of(B - 1)[0])
            if 0 <= i - 2 < B - 1:
                finish(i - 2, parts_of(i - 2)[0])
            if 0 <= i - 1 < B:
                quantise_y(i - 1, parts_of(i - 1)[-1])
            if i == B + 1:
                for n_cols in parts_of(B - 1):
                    finish(B - 1, n_cols)
            if 0 <= i - 1 < B:
                shift_residual_scalar(i - 1)
            if 0 <= i < B:
                open_y(i)
            for pair in range(2):
                if 0 <= i < B:
                    aggregate(i, 2 * pair)
                    aggregate(i, 2 * pair + 1)
                if pair == 1 and i > 0:
                    for b in regrouped:
                        regroup_tensor(b)
                if pair == 1 and 0 <= i - 1 < B:
                    for n_cols in parts_of(i - 1):
                        project(i - 1, n_cols)
                if i + 2 < B:
                    transpose_affinity(i + 2, pair)
            if 0 <= i + 1 < B:
                quantise_ag(i + 1)
            for b in regrouped:
                if i <= 0:
                    regroup_tensor(b)
                regroup_vector(b)
                if b == 2:
                    permute_weight()
            if 0 <= i < B:
                shift_residual_gpsimd(i, min(i + 1, B - 1))

        vecs = consts.tile([P, 5, 16], BF16)
        for v, vec in enumerate((w_b, bn_gamma, bn_beta, bn_mean, bn_var)):
            queue = nc.gpsimd if v % 2 == 0 and v < 4 else nc.scalar
            queue.dma_start(out=vecs[:, v, 0:HALVES], in_=vec.rearrange("(p h) -> p h", h=HALVES))

        w_codes_raw = consts.tile([P, C], I32)
        w_plane_raw = consts.tile([P, C], U8)
        w_codes = consts.tile([P, C], I32, align_bytes=64)
        w_plane = consts.tile([P, C], U8, align_bytes=64)
        nc.vector.memset(w_plane_raw[:].bitcast(I32), 0)
        for j in range(3):
            issue_loads(j)
        nc.sync.dma_start(
            out=w_codes_raw[:], in_=w_w_words[0].rearrange("p n t -> p (n t)").bitcast(I32)
        )
        for quad in range(4):
            nc.sync.dma_start(
                out=w_plane_raw[32 * quad : 32 * quad + 4, :].bitcast(I32),
                in_=w_w_scales[0, 4 * quad : 4 * quad + 4, :].bitcast(I32),
            )
        for j in range(3, LOOKAHEAD):
            issue_loads(j)

        bias_c, gamma_c, beta_c, mean_c, var_c = (vecs[:, v, 0:HALVES] for v in range(5))
        scale = consts.tile([P, HALVES], F32)
        shift = consts.tile([P, HALVES], F32)
        minus_half = consts.tile([P, HALVES], F32)
        marker = consts.tile([P, 1], U32)
        nc.gpsimd.memset(minus_half[:], -0.5)
        nc.gpsimd.tensor_scalar(out=scale[:], in0=var_c, scalar1=EPS, scalar2=None, op0=ALU.add)
        nc.gpsimd.tensor_tensor(out=scale[:], in0=scale[:], in1=minus_half[:], op=ALU.pow)
        nc.gpsimd.tensor_tensor(out=scale[:], in0=scale[:], in1=gamma_c, op=ALU.mult)
        nc.gpsimd.tensor_tensor(out=shift[:], in0=bias_c, in1=mean_c, op=ALU.subtract)
        nc.gpsimd.tensor_tensor(out=shift[:], in0=shift[:], in1=scale[:], op=ALU.mult)
        nc.gpsimd.tensor_tensor(out=shift[:], in0=shift[:], in1=beta_c, op=ALU.add)


        for i in range(-2, B + 2):
            step(i)
